import numpy as np
import ml_dtypes


def mxq(x, axis, fmt="e4m3"):
    dtype, down = {"e4m3": (ml_dtypes.float8_e4m3fn, 7), "e5m2": (ml_dtypes.float8_e5m2, 14)}[fmt]
    v = np.moveaxis(np.asarray(x, np.float32).astype(ml_dtypes.bfloat16).astype(np.float64), axis, -1)
    blocks = v.reshape(v.shape[:-1] + (-1, 32))
    amax = np.abs(blocks).max(-1, keepdims=True)
    byte = np.maximum(np.where(amax > 0, np.frexp(amax)[1] - 1 + 127, 0) - down, 1)
    scale = np.exp2(byte - 127.0)
    codes = (blocks / scale).astype(np.float32).astype(dtype).astype(np.float64)
    return np.moveaxis((codes * scale).reshape(v.shape), -1, axis)


BF16 = ml_dtypes.bfloat16


def bf(x):
    return np.asarray(x, np.float32).astype(BF16)


def f64(x):
    return np.asarray(x).astype(np.float64)


B, C, H, W, R = 8, 512, 32, 16, 4
N = H * W
EPS = 1e-12
NOISE = 0.5


def mix(a, z):
    return sum(a[:, :, r, None] * z[:, r, None, :] for r in range(R))


def l2norm(x):
    n = np.sqrt((x * x).sum(2, keepdims=True))
    return x / np.maximum(n, EPS)


def setup_inputs():
    z = np.random.standard_normal((B, R, N))
    a1 = np.random.standard_normal((B, C, R)) / np.sqrt(R)
    a2 = np.random.standard_normal((B, C, R)) / np.sqrt(R)
    x1 = mix(a1, z) + NOISE * np.random.standard_normal((B, C, N))
    x2 = mix(a2, z) + NOISE * np.random.standard_normal((B, C, N))
    return {"x1": bf(x1.reshape(B, C, H, W)), "x2": bf(x2.reshape(B, C, H, W))}


def reference(x1, x2):
    x111 = f64(x1).reshape(B, C, N)
    x211 = f64(x2).reshape(B, C, N)
    x11 = mxq(l2norm(x111), 2, "e4m3")
    x21 = mxq(l2norm(x211), 2, "e4m3")
    attn1 = x11 @ x11.transpose(0, 2, 1)
    attn2 = x21 @ x21.transpose(0, 2, 1)
    attn0 = x21 @ x11.transpose(0, 2, 1)
    attn00 = x11 @ x21.transpose(0, 2, 1)
    return attn1 + attn0, attn2 + attn00

@@ -1,0 +1,146 @@
+from contextlib import ExitStack
+
+import concourse.mybir as mybir
+from concourse.masks import make_identity
+
+F32 = mybir.dt.float32
+BF16 = mybir.dt.bfloat16
+U32 = mybir.dt.uint32
+U8 = mybir.dt.uint8
+FP8X4 = mybir.dt.float8_e4m3fn_x4
+ACT = mybir.ActivationFunctionType
+
+P = 128
+BATCH = 8
+STREAMS = 2
+CHANNELS = 512
+POSITIONS = 512
+BLOCKS = CHANNELS // P
+RUN = 2
+GROUPS = BLOCKS // RUN
+UNIT_COLS = BLOCKS * POSITIONS
+PAIRS = POSITIONS // 2
+HALVES = PAIRS // P
+BANK_BLOCKS = 2
+BANKS = BLOCKS // BANK_BLOCKS
+EPS = 1e-12
+
+FLOPS = 2 * BATCH * 4 * CHANNELS * CHANNELS * POSITIONS
+
+
+def tile_interfusion_pa_t_kernel(tc, x1, x2, out_0, out_1):
+    nc = tc.nc
+    x_views = [
+        x.rearrange("b (g p r) h w -> p b g (r h w)", g=GROUPS, r=RUN) for x in (x1, x2)
+    ]
+    out_views = [
+        o.rearrange("b (g p r) d -> p b g (r d)", g=GROUPS, r=RUN) for o in (out_0, out_1)
+    ]
+
+    with ExitStack() as stack:
+        const = stack.enter_context(tc.tile_pool(name="const", bufs=1))
+        x_pool = stack.enter_context(tc.tile_pool(name="x", bufs=BATCH * STREAMS))
+        stat_pool = stack.enter_context(tc.tile_pool(name="stat", bufs=6))
+        work_pool = stack.enter_context(tc.tile_pool(name="work", bufs=3))
+        mx_pool = stack.enter_context(tc.tile_pool(name="mx", bufs=6))
+        out_pool = stack.enter_context(tc.tile_pool(name="outs", bufs=3))
+        word_psum = stack.enter_context(tc.psum_pool(name="word_psum", bufs=4))
+        acc_psum = stack.enter_context(tc.psum_pool(name="acc_psum", bufs=4))
+
+        x_tiles = {}
+        for batch in range(BATCH):
+            for stream in range(STREAMS):
+                x_sb = x_pool.tile([P, UNIT_COLS], BF16)
+                nc.sync.dma_start(
+                    out=x_sb[:].rearrange("p (g n) -> p g n", g=GROUPS),
+                    in_=x_views[stream][:, batch, :, :],
+                )
+                x_tiles[(batch, stream)] = x_sb
+
+        identity = const.tile([P, P], F32)
+        make_identity(nc, identity[:])
+
+        one = const.tile([P, 1], F32)
+        nc.vector.memset(one[:], 1.0)
+        root_of_one = const.tile([P, 1], F32)
+        nc.scalar.activation(out=root_of_one[:], in_=one[:], func=ACT.Sqrt)
+
+        def block_cols(i):
+            return slice(i * POSITIONS, (i + 1) * POSITIONS)
+
+        def normalise(x_sb):
+            sum_sq = stat_pool.tile([P, BLOCKS], F32)
+            squares = work_pool.tile([P, UNIT_COLS], BF16)
+            for i in range(BLOCKS):
+                nc.scalar.activation(
+                    out=squares[:, block_cols(i)],
+                    in_=x_sb[:, block_cols(i)],
+                    func=ACT.Square,
+                    accum_out=sum_sq[:, i : i + 1],
+                )
+            floor_sq = stat_pool.tile([P, BLOCKS], F32)
+            nc.gpsimd.tensor_scalar_max(out=floor_sq[:], in0=sum_sq[:], scalar1=EPS * EPS)
+            norm = stat_pool.tile([P, BLOCKS], F32)
+            nc.scalar.activation(out=norm[:], in_=floor_sq[:], func=ACT.Sqrt)
+            inverse = stat_pool.tile([P, BLOCKS], F32)
+            nc.vector.reciprocal(out=inverse[:], in_=norm[:])
+            u_sb = work_pool.tile([P, UNIT_COLS], BF16)
+            for i in range(BLOCKS):
+                nc.vector.tensor_scalar_mul(
+                    out=u_sb[:, block_cols(i)],
+                    in0=x_sb[:, block_cols(i)],
+                    scalar1=inverse[:, i : i + 1],
+                )
+            return u_sb
+
+        def quantise(u_sb):
+            u_words = u_sb[:].bitcast(F32)
+            grouped = work_pool.tile([P, UNIT_COLS], BF16, align_bytes=64)
+            bank_words = BANK_BLOCKS * P * HALVES
+            for bank in range(BANKS):
+                word_bank = word_psum.tile([P, BANK_BLOCKS, HALVES, P], F32)
+                for j in range(BANK_BLOCKS):
+                    for h in range(HALVES):
+                        first = (bank * BANK_BLOCKS + j) * PAIRS + h * P
+                        nc.tensor.transpose(
+                            out=word_bank[:, j, h, :],
+                            in_=u_words[:, first : first + P],
+                            identity=identity[:],
+                        )
+                nc.vector.tensor_copy(
+                    out=grouped[:]
+                    .bitcast(F32)[:, bank * bank_words : (bank + 1) * bank_words]
+                    .rearrange("q (j c h) -> q j c h", j=BANK_BLOCKS, h=HALVES),
+                    in_=word_bank[:].rearrange("q j h c -> q j c h"),
+                )
+            codes = mx_pool.tile([P, CHANNELS], U32, align_bytes=64)
+            scales = mx_pool.tile([P, CHANNELS], U8, align_bytes=64)
+            nc.vector.quantize_mx(out=codes[:].bitcast(FP8X4), scales=scales[:], in_=grouped[:])
+            return codes, scales
+
+        def products(own, other, out_rows):
+            stage = out_pool.tile([P, BLOCKS * CHANNELS], F32)
+            for i in range(BLOCKS):
+                acc = acc_psum.tile([P, CHANNELS], F32)
+                for left in (own, other):
+                    nc.tensor.matmul_mx(
+                        out=acc[:],
+                        lhsT=left[0][:, i * P : (i + 1) * P].bitcast(FP8X4),
+                        lhsT_scale=left[1][:, i * P : (i + 1) * P],
+                        rhs=own[0][:].bitcast(FP8X4),
+                        rhs_scale=own[1][:],
+                        start=(left is own),
+                        stop=(left is other),
+                    )
+                nc.any.tensor_copy(
+                    out=stage[:, i * CHANNELS : (i + 1) * CHANNELS].rearrange(
+                        "p (g c r) -> p g c r", g=GROUPS, r=RUN
+                    ),
+                    in_=acc[:].rearrange("p (g r c) -> p g c r", g=GROUPS, r=RUN),
+                )
+            nc.sync.dma_start(out=out_rows, in_=stage[:].rearrange("p (g n) -> p g n", g=GROUPS))
+
+        for batch in range(BATCH):
+            quantised = [quantise(normalise(x_tiles[(batch, stream)])) for stream in range(STREAMS)]
+            for stream in range(STREAMS):
+                products(quantised[stream], quantised[1 - stream], out_views[stream][:, batch, :, :])

@@ -9,20 +9,20 @@ U32 = mybir.dt.uint32
 U8 = mybir.dt.uint8
 FP8X4 = mybir.dt.float8_e4m3fn_x4
 ACT = mybir.ActivationFunctionType
+ALU = mybir.AluOpType
 
 P = 128
 BATCH = 8
 STREAMS = 2
+UNITS = BATCH * STREAMS
 CHANNELS = 512
 POSITIONS = 512
 BLOCKS = CHANNELS // P
 RUN = 2
 GROUPS = BLOCKS // RUN
-UNIT_COLS = BLOCKS * POSITIONS
+HALF_COLS = RUN * POSITIONS
 PAIRS = POSITIONS // 2
 HALVES = PAIRS // P
-BANK_BLOCKS = 2
-BANKS = BLOCKS // BANK_BLOCKS
 EPS = 1e-12
 
 FLOPS = 2 * BATCH * 4 * CHANNELS * CHANNELS * POSITIONS
@@ -39,108 +39,204 @@ def tile_interfusion_pa_t_kernel(tc, x1, x2, out_0, out_1):
 
     with ExitStack() as stack:
         const = stack.enter_context(tc.tile_pool(name="const", bufs=1))
-        x_pool = stack.enter_context(tc.tile_pool(name="x", bufs=BATCH * STREAMS))
-        stat_pool = stack.enter_context(tc.tile_pool(name="stat", bufs=6))
+        x_pool = stack.enter_context(tc.tile_pool(name="x", bufs=UNITS * GROUPS))
+        stat_pool = stack.enter_context(tc.tile_pool(name="stat", bufs=4))
         work_pool = stack.enter_context(tc.tile_pool(name="work", bufs=3))
         mx_pool = stack.enter_context(tc.tile_pool(name="mx", bufs=6))
-        out_pool = stack.enter_context(tc.tile_pool(name="outs", bufs=3))
+        out_pool = stack.enter_context(tc.tile_pool(name="outs", bufs=6))
         word_psum = stack.enter_context(tc.psum_pool(name="word_psum", bufs=4))
         acc_psum = stack.enter_context(tc.psum_pool(name="acc_psum", bufs=4))
+        stack.enter_context(tc.manual_schedule())
 
         x_tiles = {}
-        for batch in range(BATCH):
-            for stream in range(STREAMS):
-                x_sb = x_pool.tile([P, UNIT_COLS], BF16)
+        for unit in range(UNITS):
+            for g in range(GROUPS):
+                x_sb = x_pool.tile([P, HALF_COLS], BF16)
                 nc.sync.dma_start(
-                    out=x_sb[:].rearrange("p (g n) -> p g n", g=GROUPS),
-                    in_=x_views[stream][:, batch, :, :],
+                    out=x_sb[:], in_=x_views[unit % STREAMS][:, unit // STREAMS, g, :]
                 )
-                x_tiles[(batch, stream)] = x_sb
+                x_tiles[(unit, g)] = x_sb
 
-        identity = const.tile([P, P], F32)
-        make_identity(nc, identity[:])
+        def x_block(unit, i):
+            r = i % RUN
+            return x_tiles[(unit, i // RUN)][:, r * POSITIONS : (r + 1) * POSITIONS]
 
         one = const.tile([P, 1], F32)
         nc.vector.memset(one[:], 1.0)
         root_of_one = const.tile([P, 1], F32)
         nc.scalar.activation(out=root_of_one[:], in_=one[:], func=ACT.Sqrt)
 
-        def block_cols(i):
-            return slice(i * POSITIONS, (i + 1) * POSITIONS)
+        identity = const.tile([P, P], F32)
+        make_identity(nc, identity[:])
 
-        def normalise(x_sb):
-            sum_sq = stat_pool.tile([P, BLOCKS], F32)
-            squares = work_pool.tile([P, UNIT_COLS], BF16)
-            for i in range(BLOCKS):
-                nc.scalar.activation(
-                    out=squares[:, block_cols(i)],
-                    in_=x_sb[:, block_cols(i)],
-                    func=ACT.Square,
-                    accum_out=sum_sq[:, i : i + 1],
+        sums, norms, inverses, u_tiles, word_banks, grouped_tiles = {}, {}, {}, {}, {}, {}
+        quantised, accs, stages = {}, {}, {}
+
+        def square(unit, i, on_vector=False):
+            if i == 0:
+                sums[unit] = stat_pool.tile([P, BLOCKS], F32, name="sum_sq")
+            x = x_block(unit, i)
+            total = sums[unit][:, i : i + 1]
+            if on_vector:
+                squares_v = work_pool.tile([P, POSITIONS], BF16)
+                nc.vector.scalar_tensor_tensor(
+                    out=squares_v[:], in0=x, scalar=1.0, in1=x,
+                    op0=ALU.mult, op1=ALU.mult, accum_out=total,
                 )
+            else:
+                squares_s = work_pool.tile([P, POSITIONS], BF16)
+                nc.scalar.activation(out=squares_s[:], in_=x, func=ACT.Square, accum_out=total)
+
+        def norm(unit):
             floor_sq = stat_pool.tile([P, BLOCKS], F32)
-            nc.gpsimd.tensor_scalar_max(out=floor_sq[:], in0=sum_sq[:], scalar1=EPS * EPS)
-            norm = stat_pool.tile([P, BLOCKS], F32)
-            nc.scalar.activation(out=norm[:], in_=floor_sq[:], func=ACT.Sqrt)
+            nc.gpsimd.tensor_scalar_max(out=floor_sq[:], in0=sums[unit][:], scalar1=EPS * EPS)
+            norms[unit] = stat_pool.tile([P, BLOCKS], F32, name="norm_sb")
+            nc.scalar.activation(out=norms[unit][:], in_=floor_sq[:], func=ACT.Sqrt)
+
+        def invert(unit):
             inverse = stat_pool.tile([P, BLOCKS], F32)
-            nc.vector.reciprocal(out=inverse[:], in_=norm[:])
-            u_sb = work_pool.tile([P, UNIT_COLS], BF16)
+            nc.vector.reciprocal(out=inverse[:], in_=norms[unit][:])
+            inverses[unit] = inverse
+
+        def scale(unit):
+            u_sb = work_pool.tile([P, BLOCKS, POSITIONS], BF16)
             for i in range(BLOCKS):
                 nc.vector.tensor_scalar_mul(
-                    out=u_sb[:, block_cols(i)],
-                    in0=x_sb[:, block_cols(i)],
-                    scalar1=inverse[:, i : i + 1],
+                    out=u_sb[:, i, :],
+                    in0=x_block(unit, i),
+                    scalar1=inverses[unit][:, i : i + 1],
                 )
-            return u_sb
+            u_tiles[unit] = u_sb
 
-        def quantise(u_sb):
-            u_words = u_sb[:].bitcast(F32)
-            grouped = work_pool.tile([P, UNIT_COLS], BF16, align_bytes=64)
-            bank_words = BANK_BLOCKS * P * HALVES
-            for bank in range(BANKS):
-                word_bank = word_psum.tile([P, BANK_BLOCKS, HALVES, P], F32)
-                for j in range(BANK_BLOCKS):
+        def transpose(unit):
+            banks = []
+            for g in range(GROUPS):
+                word_bank = word_psum.tile([P, RUN, HALVES, P], F32)
+                for r in range(RUN):
+                    words = u_tiles[unit][:, g * RUN + r, :].bitcast(F32)
                     for h in range(HALVES):
-                        first = (bank * BANK_BLOCKS + j) * PAIRS + h * P
                         nc.tensor.transpose(
-                            out=word_bank[:, j, h, :],
-                            in_=u_words[:, first : first + P],
+                            out=word_bank[:, r, h, :],
+                            in_=words[:, h * P : (h + 1) * P],
                             identity=identity[:],
                         )
-                nc.vector.tensor_copy(
-                    out=grouped[:]
-                    .bitcast(F32)[:, bank * bank_words : (bank + 1) * bank_words]
-                    .rearrange("q (j c h) -> q j c h", j=BANK_BLOCKS, h=HALVES),
-                    in_=word_bank[:].rearrange("q j h c -> q j c h"),
+                banks.append(word_bank)
+            word_banks[unit] = banks
+
+        def gather_words(unit, g, copy):
+            if g == 0:
+                grouped_tiles[unit] = work_pool.tile(
+                    [P, BLOCKS, P, HALVES * 2], BF16, name="grouped", align_bytes=64
                 )
+            copy(
+                out=grouped_tiles[unit][:, g * RUN : (g + 1) * RUN, :, :].bitcast(F32),
+                in_=word_banks[unit][g][:].rearrange("q j h c -> q j c h"),
+            )
+
+        def quantise(unit):
             codes = mx_pool.tile([P, CHANNELS], U32, align_bytes=64)
             scales = mx_pool.tile([P, CHANNELS], U8, align_bytes=64)
-            nc.vector.quantize_mx(out=codes[:].bitcast(FP8X4), scales=scales[:], in_=grouped[:])
-            return codes, scales
+            nc.vector.quantize_mx(
+                out=codes[:].bitcast(FP8X4),
+                scales=scales[:],
+                in_=grouped_tiles[unit][:].rearrange("q j c k -> q (j c k)"),
+            )
+            quantised[unit] = (codes, scales)
 
-        def products(own, other, out_rows):
-            stage = out_pool.tile([P, BLOCKS * CHANNELS], F32)
-            for i in range(BLOCKS):
-                acc = acc_psum.tile([P, CHANNELS], F32)
-                for left in (own, other):
-                    nc.tensor.matmul_mx(
-                        out=acc[:],
-                        lhsT=left[0][:, i * P : (i + 1) * P].bitcast(FP8X4),
-                        lhsT_scale=left[1][:, i * P : (i + 1) * P],
-                        rhs=own[0][:].bitcast(FP8X4),
-                        rhs_scale=own[1][:],
-                        start=(left is own),
-                        stop=(left is other),
-                    )
-                nc.any.tensor_copy(
-                    out=stage[:, i * CHANNELS : (i + 1) * CHANNELS].rearrange(
-                        "p (g c r) -> p g c r", g=GROUPS, r=RUN
-                    ),
-                    in_=acc[:].rearrange("p (g r c) -> p g c r", g=GROUPS, r=RUN),
+        def multiply(unit, i, left_unit):
+            own, left = quantised[unit], quantised[left_unit]
+            if left_unit == unit:
+                accs[(unit, i)] = acc_psum.tile([P, CHANNELS], F32, name="acc")
+            nc.tensor.matmul_mx(
+                out=accs[(unit, i)][:],
+                lhsT=left[0][:, i * P : (i + 1) * P].bitcast(FP8X4),
+                lhsT_scale=left[1][:, i * P : (i + 1) * P],
+                rhs=own[0][:].bitcast(FP8X4),
+                rhs_scale=own[1][:],
+                start=(left_unit == unit),
+                stop=(left_unit != unit),
+            )
+
+        def copy_out(unit, i, copy):
+            acc = accs[(unit, i)]
+            g, r = i // RUN, i % RUN
+            if r == 0:
+                stages[(unit, g)] = out_pool.tile([P, RUN, CHANNELS], F32, name="stage")
+            stage = stages[(unit, g)]
+            copy(
+                out=stage[:, r, :].rearrange("p (g c r) -> p g c r", g=GROUPS, r=RUN),
+                in_=acc[:].rearrange("p (g r c) -> p g c r", g=GROUPS, r=RUN),
+            )
+            if r == RUN - 1:
+                nc.sync.dma_start(
+                    out=out_views[unit % STREAMS][:, unit // STREAMS, g, :],
+                    in_=stage[:].rearrange("p r n -> p (r n)"),
                 )
-            nc.sync.dma_start(out=out_rows, in_=stage[:].rearrange("p (g n) -> p g n", g=GROUPS))
 
-        for batch in range(BATCH):
-            quantised = [quantise(normalise(x_tiles[(batch, stream)])) for stream in range(STREAMS)]
-            for stream in range(STREAMS):
-                products(quantised[stream], quantised[1 - stream], out_views[stream][:, batch, :, :])
+        on_vector, on_scalar = nc.vector.tensor_copy, nc.scalar.copy
+
+        square(0, 0)
+        square(0, 1, on_vector=True)
+        square(0, 2)
+        square(0, 3, on_vector=True)
+        square(1, 0)
+        norm(0)
+        square(1, 1, on_vector=True)
+        invert(0)
+        scale(0)
+        transpose(0)
+        square(1, 2)
+        square(1, 3, on_vector=True)
+        square(2, 0)
+        square(2, 1)
+        norm(1)
+        gather_words(0, 0, on_vector)
+        gather_words(0, 1, on_scalar)
+        invert(1)
+        scale(1)
+        transpose(1)
+        quantise(0)
+        square(2, 2)
+        gather_words(1, 0, on_vector)
+        gather_words(1, 1, on_scalar)
+        square(2, 3)
+        square(3, 0)
+        norm(2)
+        square(3, 1)
+        invert(2)
+
+        for t in range(UNITS + 1):
+            product = t < UNITS
+            if product:
+                for i in range(BLOCKS - 1):
+                    multiply(t, i, t)
+            if t + 2 < UNITS:
+                scale(t + 2)
+            if t > 0:
+                copy_out(t - 1, 3, on_vector)
+            if t + 3 < UNITS:
+                square(t + 3, 2)
+                square(t + 3, 3)
+            if t + 2 < UNITS:
+                transpose(t + 2)
+            if t + 1 < UNITS:
+                quantise(t + 1)
+            if t + 4 < UNITS:
+                square(t + 4, 0)
+            if t + 3 < UNITS:
+                norm(t + 3)
+            if t + 4 < UNITS:
+                square(t + 4, 1)
+            if t + 2 < UNITS:
+                gather_words(t + 2, 0, on_vector)
+                gather_words(t + 2, 1, on_vector if t + 3 < UNITS else on_scalar)
+            if t + 3 < UNITS:
+                invert(t + 3)
+            if product:
+                for i in range(BLOCKS):
+                    if i == BLOCKS - 1:
+                        multiply(t, i, t)
+                    multiply(t, i, t ^ 1)
+                copy_out(t, 0, on_vector if t == 0 else on_scalar)
+                copy_out(t, 1, on_vector)
+                copy_out(t, 2, on_scalar)

@@ -44,17 +44,21 @@ def tile_interfusion_pa_t_kernel(tc, x1, x2, out_0, out_1):
         work_pool = stack.enter_context(tc.tile_pool(name="work", bufs=3))
         mx_pool = stack.enter_context(tc.tile_pool(name="mx", bufs=6))
         out_pool = stack.enter_context(tc.tile_pool(name="outs", bufs=6))
-        word_psum = stack.enter_context(tc.psum_pool(name="word_psum", bufs=4))
-        acc_psum = stack.enter_context(tc.psum_pool(name="acc_psum", bufs=4))
+        word_psum = stack.enter_context(tc.psum_pool(name="word_psum", bufs=3))
+        acc_psum = stack.enter_context(tc.psum_pool(name="acc_psum", bufs=5))
         stack.enter_context(tc.manual_schedule())
 
         x_tiles = {}
         for unit in range(UNITS):
             for g in range(GROUPS):
                 x_sb = x_pool.tile([P, HALF_COLS], BF16)
-                nc.sync.dma_start(
-                    out=x_sb[:], in_=x_views[unit % STREAMS][:, unit // STREAMS, g, :]
-                )
+                x_rows = x_views[unit % STREAMS][:, unit // STREAMS, g, :]
+                if unit == 0:
+                    for r in range(RUN):
+                        cols = slice(r * POSITIONS, (r + 1) * POSITIONS)
+                        nc.sync.dma_start(out=x_sb[:, cols], in_=x_rows[:, cols])
+                else:
+                    nc.sync.dma_start(out=x_sb[:], in_=x_rows)
                 x_tiles[(unit, g)] = x_sb
 
         def x_block(unit, i):
@@ -66,14 +70,19 @@ def tile_interfusion_pa_t_kernel(tc, x1, x2, out_0, out_1):
         root_of_one = const.tile([P, 1], F32)
         nc.scalar.activation(out=root_of_one[:], in_=one[:], func=ACT.Sqrt)
 
+        plus_floor = const.tile([P, 1], F32)
+        nc.vector.tensor_scalar_mul(out=plus_floor[:], in0=one[:], scalar1=EPS * EPS)
+        minus_floor = const.tile([P, 1], F32)
+        nc.vector.tensor_scalar_mul(out=minus_floor[:], in0=one[:], scalar1=-EPS * EPS)
+
         identity = const.tile([P, P], F32)
         make_identity(nc, identity[:])
 
-        sums, norms, inverses, u_tiles, word_banks, grouped_tiles = {}, {}, {}, {}, {}, {}
-        quantised, accs, stages = {}, {}, {}
+        sums, excesses, norms, inverses, u_tiles = {}, {}, {}, {}, {}
+        word_banks, grouped_tiles, quantised, accs, stages = {}, {}, {}, {}, {}
 
         def square(unit, i, on_vector=False):
-            if i == 0:
+            if unit not in sums:
                 sums[unit] = stat_pool.tile([P, BLOCKS], F32, name="sum_sq")
             x = x_block(unit, i)
             total = sums[unit][:, i : i + 1]
@@ -87,11 +96,17 @@ def tile_interfusion_pa_t_kernel(tc, x1, x2, out_0, out_1):
                 squares_s = work_pool.tile([P, POSITIONS], BF16)
                 nc.scalar.activation(out=squares_s[:], in_=x, func=ACT.Square, accum_out=total)
 
+        def clamp(unit):
+            excesses[unit] = stat_pool.tile([P, BLOCKS], F32, name="excess")
+            nc.scalar.activation(
+                out=excesses[unit][:], in_=sums[unit][:], func=ACT.Relu, bias=minus_floor[:]
+            )
+
         def norm(unit):
-            floor_sq = stat_pool.tile([P, BLOCKS], F32)
-            nc.gpsimd.tensor_scalar_max(out=floor_sq[:], in0=sums[unit][:], scalar1=EPS * EPS)
             norms[unit] = stat_pool.tile([P, BLOCKS], F32, name="norm_sb")
-            nc.scalar.activation(out=norms[unit][:], in_=floor_sq[:], func=ACT.Sqrt)
+            nc.scalar.activation(
+                out=norms[unit][:], in_=excesses[unit][:], func=ACT.Sqrt, bias=plus_floor[:]
+            )
 
         def invert(unit):
             inverse = stat_pool.tile([P, BLOCKS], F32)
@@ -124,7 +139,7 @@ def tile_interfusion_pa_t_kernel(tc, x1, x2, out_0, out_1):
             word_banks[unit] = banks
 
         def gather_words(unit, g, copy):
-            if g == 0:
+            if unit not in grouped_tiles:
                 grouped_tiles[unit] = work_pool.tile(
                     [P, BLOCKS, P, HALVES * 2], BF16, name="grouped", align_bytes=64
                 )
@@ -167,11 +182,13 @@ def tile_interfusion_pa_t_kernel(tc, x1, x2, out_0, out_1):
                 out=stage[:, r, :].rearrange("p (g c r) -> p g c r", g=GROUPS, r=RUN),
                 in_=acc[:].rearrange("p (g r c) -> p g c r", g=GROUPS, r=RUN),
             )
-            if r == RUN - 1:
+            out_rows = out_views[unit % STREAMS][:, unit // STREAMS, g, :]
+            if unit == UNITS - 1:
                 nc.sync.dma_start(
-                    out=out_views[unit % STREAMS][:, unit // STREAMS, g, :],
-                    in_=stage[:].rearrange("p r n -> p (r n)"),
+                    out=out_rows[:, r * CHANNELS : (r + 1) * CHANNELS], in_=stage[:, r, :]
                 )
+            elif r == RUN - 1:
+                nc.sync.dma_start(out=out_rows, in_=stage[:].rearrange("p r n -> p (r n)"))
 
         on_vector, on_scalar = nc.vector.tensor_copy, nc.scalar.copy
 
@@ -180,63 +197,111 @@ def tile_interfusion_pa_t_kernel(tc, x1, x2, out_0, out_1):
         square(0, 2)
         square(0, 3, on_vector=True)
         square(1, 0)
-        norm(0)
         square(1, 1, on_vector=True)
+        clamp(0)
+        square(1, 2)
+        norm(0)
+        square(1, 3, on_vector=True)
         invert(0)
+        square(2, 0)
+        square(2, 1, on_vector=True)
         scale(0)
         transpose(0)
-        square(1, 2)
-        square(1, 3, on_vector=True)
-        square(2, 0)
-        square(2, 1)
+        square(2, 2)
+        clamp(1)
+        square(2, 3)
         norm(1)
-        gather_words(0, 0, on_vector)
-        gather_words(0, 1, on_scalar)
+        square(3, 3, on_vector=True)
+        gather_words(0, 1, on_vector)
         invert(1)
         scale(1)
+        gather_words(0, 0, on_scalar)
         transpose(1)
-        quantise(0)
-        square(2, 2)
-        gather_words(1, 0, on_vector)
-        gather_words(1, 1, on_scalar)
-        square(2, 3)
+        clamp(2)
         square(3, 0)
         norm(2)
-        square(3, 1)
+        quantise(0)
         invert(2)
+        square(3, 1)
+        gather_words(1, 1, on_vector)
+        square(3, 2)
+        multiply(0, 0, 0)
+        multiply(0, 1, 0)
+        multiply(0, 2, 0)
+        clamp(3)
+        scale(2)
+        gather_words(1, 0, on_scalar)
+        quantise(1)
+        transpose(2)
+        square(4, 0)
+        norm(3)
+        multiply(0, 0, 1)
+        multiply(0, 1, 1)
+        multiply(0, 2, 1)
+        multiply(0, 3, 0)
+        multiply(0, 3, 1)
+        invert(3)
+        scale(3)
+        square(4, 1)
+        gather_words(2, 0, on_vector)
+        copy_out(0, 0, on_scalar)
+        multiply(1, 0, 1)
+        multiply(1, 1, 1)
+        multiply(1, 0, 0)
+        multiply(1, 1, 0)
+        gather_words(2, 1, on_vector)
+        transpose(3)
+        copy_out(0, 1, on_scalar)
+        multiply(1, 2, 1)
+        multiply(1, 2, 0)
+        square(4, 2)
+        square(4, 3)
+        copy_out(0, 2, on_vector)
+        multiply(1, 3, 1)
+        multiply(1, 3, 0)
+        clamp(4)
+        square(5, 0)
+        norm(4)
+        copy_out(0, 3, on_vector)
+        quantise(2)
+        invert(4)
+        gather_words(3, 0, on_scalar)
+        gather_words(3, 1, on_scalar)
+        square(5, 1)
+        copy_out(1, 0, on_vector)
+        copy_out(1, 1, on_vector)
 
-        for t in range(UNITS + 1):
-            product = t < UNITS
-            if product:
+        for t in range(2, UNITS + 1):
+            if t < UNITS:
                 for i in range(BLOCKS - 1):
                     multiply(t, i, t)
             if t + 2 < UNITS:
                 scale(t + 2)
-            if t > 0:
-                copy_out(t - 1, 3, on_vector)
-            if t + 3 < UNITS:
-                square(t + 3, 2)
-                square(t + 3, 3)
-            if t + 2 < UNITS:
                 transpose(t + 2)
             if t + 1 < UNITS:
                 quantise(t + 1)
+            copy_out(t - 1, 2, on_scalar if t - 1 >= UNITS - 4 else on_vector)
+            copy_out(t - 1, 3, on_vector)
+            if t + 3 < UNITS:
+                square(t + 3, 2)
+                square(t + 3, 3)
+                clamp(t + 3)
             if t + 4 < UNITS:
                 square(t + 4, 0)
             if t + 3 < UNITS:
                 norm(t + 3)
+            if t + 2 < UNITS:
+                gather_words(t + 2, 0, on_vector if t + 2 >= UNITS - 2 else on_scalar)
+                gather_words(t + 2, 1, on_scalar)
             if t + 4 < UNITS:
                 square(t + 4, 1)
-            if t + 2 < UNITS:
-                gather_words(t + 2, 0, on_vector)
-                gather_words(t + 2, 1, on_vector if t + 3 < UNITS else on_scalar)
-            if t + 3 < UNITS:
-                invert(t + 3)
-            if product:
+            if t < UNITS:
                 for i in range(BLOCKS):
                     if i == BLOCKS - 1:
                         multiply(t, i, t)
                     multiply(t, i, t ^ 1)
-                copy_out(t, 0, on_vector if t == 0 else on_scalar)
+                copy_out(t, 0, on_scalar if t >= UNITS - 4 else on_vector)
+            if t + 3 < UNITS:
+                invert(t + 3)
+            if t < UNITS:
                 copy_out(t, 1, on_vector)
-                copy_out(t, 2, on_scalar)

@@ -228,9 +228,9 @@ def tile_interfusion_pa_t_kernel(tc, x1, x2, out_0, out_1):
         multiply(0, 0, 0)
         multiply(0, 1, 0)
         multiply(0, 2, 0)
-        clamp(3)
         scale(2)
         gather_words(1, 0, on_scalar)
+        clamp(3)
         quantise(1)
         transpose(2)
         square(4, 0)
@@ -244,6 +244,7 @@ def tile_interfusion_pa_t_kernel(tc, x1, x2, out_0, out_1):
         scale(3)
         square(4, 1)
         gather_words(2, 0, on_vector)
+        square(4, 2)
         copy_out(0, 0, on_scalar)
         multiply(1, 0, 1)
         multiply(1, 1, 1)
@@ -254,21 +255,20 @@ def tile_interfusion_pa_t_kernel(tc, x1, x2, out_0, out_1):
         copy_out(0, 1, on_scalar)
         multiply(1, 2, 1)
         multiply(1, 2, 0)
-        square(4, 2)
         square(4, 3)
         copy_out(0, 2, on_vector)
         multiply(1, 3, 1)
         multiply(1, 3, 0)
-        clamp(4)
         square(5, 0)
-        norm(4)
+        clamp(4)
         copy_out(0, 3, on_vector)
         quantise(2)
-        invert(4)
         gather_words(3, 0, on_scalar)
+        norm(4)
         gather_words(3, 1, on_scalar)
         square(5, 1)
         copy_out(1, 0, on_vector)
+        invert(4)
         copy_out(1, 1, on_vector)
 
         for t in range(2, UNITS + 1):
@@ -285,13 +285,15 @@ def tile_interfusion_pa_t_kernel(tc, x1, x2, out_0, out_1):
             if t + 3 < UNITS:
                 square(t + 3, 2)
                 square(t + 3, 3)
-                clamp(t + 3)
             if t + 4 < UNITS:
                 square(t + 4, 0)
             if t + 3 < UNITS:
-                norm(t + 3)
+                clamp(t + 3)
             if t + 2 < UNITS:
                 gather_words(t + 2, 0, on_vector if t + 2 >= UNITS - 2 else on_scalar)
+            if t + 3 < UNITS:
+                norm(t + 3)
+            if t + 2 < UNITS:
                 gather_words(t + 2, 1, on_scalar)
             if t + 4 < UNITS:
                 square(t + 4, 1)

@@ -78,6 +78,16 @@ def tile_interfusion_pa_t_kernel(tc, x1, x2, out_0, out_1):
         identity = const.tile([P, P], F32)
         make_identity(nc, identity[:])
 
+        zeros = const.tile([P, CHANNELS], BF16)
+        nc.gpsimd.memset(zeros[:], 0.0)
+
+        def warm_up(count):
+            idle_bank = word_psum.tile([P, CHANNELS], F32, name="word_bank")
+            for k in range(count):
+                nc.tensor.matmul(
+                    out=idle_bank[:], lhsT=zeros[:, :P], rhs=zeros[:], start=True, stop=True
+                )
+
         sums, excesses, norms, inverses, u_tiles = {}, {}, {}, {}, {}
         word_banks, grouped_tiles, quantised, accs, stages = {}, {}, {}, {}, {}
 
@@ -192,6 +202,7 @@ def tile_interfusion_pa_t_kernel(tc, x1, x2, out_0, out_1):
 
         on_vector, on_scalar = nc.vector.tensor_copy, nc.scalar.copy
 
+        warm_up(8)
         square(0, 0)
         square(0, 1, on_vector=True)
         square(0, 2)
@@ -207,6 +218,7 @@ def tile_interfusion_pa_t_kernel(tc, x1, x2, out_0, out_1):
         square(2, 1, on_vector=True)
         scale(0)
         transpose(0)
+        warm_up(3)
         square(2, 2)
         clamp(1)
         square(2, 3)

@@ -43,7 +43,7 @@ def tile_interfusion_pa_t_kernel(tc, x1, x2, out_0, out_1):
         stat_pool = stack.enter_context(tc.tile_pool(name="stat", bufs=4))
         work_pool = stack.enter_context(tc.tile_pool(name="work", bufs=3))
         mx_pool = stack.enter_context(tc.tile_pool(name="mx", bufs=6))
-        out_pool = stack.enter_context(tc.tile_pool(name="outs", bufs=6))
+        out_pool = stack.enter_context(tc.tile_pool(name="outs", bufs=12))
         word_psum = stack.enter_context(tc.psum_pool(name="word_psum", bufs=3))
         acc_psum = stack.enter_context(tc.psum_pool(name="acc_psum", bufs=5))
         stack.enter_context(tc.manual_schedule())
@@ -200,6 +200,35 @@ def tile_interfusion_pa_t_kernel(tc, x1, x2, out_0, out_1):
             elif r == RUN - 1:
                 nc.sync.dma_start(out=out_rows, in_=stage[:].rearrange("p r n -> p (r n)"))
 
+        def last_block():
+            unit, i, half = UNITS - 1, BLOCKS - 1, CHANNELS // GROUPS
+            own, other = quantised[unit], quantised[unit ^ 1]
+            stage = stages[(unit, GROUPS - 1)]
+            for g, copy in enumerate((on_vector, on_scalar)):
+                cols = slice(g * half, (g + 1) * half)
+                acc = acc_psum.tile([P, half], F32)
+                for left in (own, other):
+                    nc.tensor.matmul_mx(
+                        out=acc[:],
+                        lhsT=left[0][:, i * P : (i + 1) * P].bitcast(FP8X4),
+                        lhsT_scale=left[1][:, i * P : (i + 1) * P],
+                        rhs=own[0][:, cols].bitcast(FP8X4),
+                        rhs_scale=own[1][:, cols],
+                        start=(left is own),
+                        stop=(left is other),
+                    )
+                copy(
+                    out=stage[:, RUN - 1, cols].rearrange("p (c r) -> p c r", r=RUN),
+                    in_=acc[:].rearrange("p (r c) -> p c r", r=RUN),
+                )
+                first = (RUN - 1) * CHANNELS + g * half
+                nc.sync.dma_start(
+                    out=out_views[unit % STREAMS][
+                        :, unit // STREAMS, GROUPS - 1, first : first + half
+                    ],
+                    in_=stage[:, RUN - 1, cols],
+                )
+
         on_vector, on_scalar = nc.vector.tensor_copy, nc.scalar.copy
 
         warm_up(8)
@@ -258,12 +287,12 @@ def tile_interfusion_pa_t_kernel(tc, x1, x2, out_0, out_1):
         gather_words(2, 0, on_vector)
         square(4, 2)
         copy_out(0, 0, on_scalar)
+        transpose(3)
         multiply(1, 0, 1)
         multiply(1, 1, 1)
         multiply(1, 0, 0)
         multiply(1, 1, 0)
         gather_words(2, 1, on_vector)
-        transpose(3)
         copy_out(0, 1, on_scalar)
         multiply(1, 2, 1)
         multiply(1, 2, 0)
@@ -293,7 +322,8 @@ def tile_interfusion_pa_t_kernel(tc, x1, x2, out_0, out_1):
             if t + 1 < UNITS:
                 quantise(t + 1)
             copy_out(t - 1, 2, on_scalar if t - 1 >= UNITS - 4 else on_vector)
-            copy_out(t - 1, 3, on_vector)
+            if t < UNITS:
+                copy_out(t - 1, 3, on_scalar if t - 1 == UNITS - 4 else on_vector)
             if t + 3 < UNITS:
                 square(t + 3, 2)
                 square(t + 3, 3)
@@ -310,7 +340,7 @@ def tile_interfusion_pa_t_kernel(tc, x1, x2, out_0, out_1):
             if t + 4 < UNITS:
                 square(t + 4, 1)
             if t < UNITS:
-                for i in range(BLOCKS):
+                for i in range(BLOCKS if t < UNITS - 1 else BLOCKS - 1):
                     if i == BLOCKS - 1:
                         multiply(t, i, t)
                     multiply(t, i, t ^ 1)
@@ -319,3 +349,4 @@ def tile_interfusion_pa_t_kernel(tc, x1, x2, out_0, out_1):
                 invert(t + 3)
             if t < UNITS:
                 copy_out(t, 1, on_vector)
+        last_block()

@@ -159,8 +159,8 @@ def tile_interfusion_pa_t_kernel(tc, x1, x2, out_0, out_1):
             )
 
         def quantise(unit):
-            codes = mx_pool.tile([P, CHANNELS], U32, align_bytes=64)
-            scales = mx_pool.tile([P, CHANNELS], U8, align_bytes=64)
+            codes = mx_pool.tile([P, CHANNELS], U32, align_bytes=256)
+            scales = mx_pool.tile([P, CHANNELS], U8, align_bytes=256)
             nc.vector.quantize_mx(
                 out=codes[:].bitcast(FP8X4),
                 scales=scales[:],
@@ -252,7 +252,7 @@ def tile_interfusion_pa_t_kernel(tc, x1, x2, out_0, out_1):
         clamp(1)
         square(2, 3)
         norm(1)
-        square(3, 3, on_vector=True)
+        square(3, 1, on_vector=True)
         gather_words(0, 1, on_vector)
         invert(1)
         scale(1)
@@ -263,7 +263,7 @@ def tile_interfusion_pa_t_kernel(tc, x1, x2, out_0, out_1):
         norm(2)
         quantise(0)
         invert(2)
-        square(3, 1)
+        square(3, 3)
         gather_words(1, 1, on_vector)
         square(3, 2)
         multiply(0, 0, 0)

@@ -231,7 +231,7 @@ def tile_interfusion_pa_t_kernel(tc, x1, x2, out_0, out_1):
 
         on_vector, on_scalar = nc.vector.tensor_copy, nc.scalar.copy
 
-        warm_up(8)
+        warm_up(12)
         square(0, 0)
         square(0, 1, on_vector=True)
         square(0, 2)

@@ -44,8 +44,8 @@ def tile_interfusion_pa_t_kernel(tc, x1, x2, out_0, out_1):
         work_pool = stack.enter_context(tc.tile_pool(name="work", bufs=3))
         mx_pool = stack.enter_context(tc.tile_pool(name="mx", bufs=6))
         out_pool = stack.enter_context(tc.tile_pool(name="outs", bufs=12))
-        word_psum = stack.enter_context(tc.psum_pool(name="word_psum", bufs=3))
-        acc_psum = stack.enter_context(tc.psum_pool(name="acc_psum", bufs=5))
+        word_psum = stack.enter_context(tc.psum_pool(name="word_psum", bufs=2))
+        acc_psum = stack.enter_context(tc.psum_pool(name="acc_psum", bufs=6))
         stack.enter_context(tc.manual_schedule())
 
         x_tiles = {}
@@ -82,7 +82,7 @@ def tile_interfusion_pa_t_kernel(tc, x1, x2, out_0, out_1):
         nc.gpsimd.memset(zeros[:], 0.0)
 
         def warm_up(count):
-            idle_bank = word_psum.tile([P, CHANNELS], F32, name="word_bank")
+            idle_bank = acc_psum.tile([P, CHANNELS], F32, name="acc")
             for k in range(count):
                 nc.tensor.matmul(
                     out=idle_bank[:], lhsT=zeros[:, :P], rhs=zeros[:], start=True, stop=True
@@ -287,12 +287,12 @@ def tile_interfusion_pa_t_kernel(tc, x1, x2, out_0, out_1):
         gather_words(2, 0, on_vector)
         square(4, 2)
         copy_out(0, 0, on_scalar)
-        transpose(3)
         multiply(1, 0, 1)
-        multiply(1, 1, 1)
         multiply(1, 0, 0)
-        multiply(1, 1, 0)
         gather_words(2, 1, on_vector)
+        transpose(3)
+        multiply(1, 1, 1)
+        multiply(1, 1, 0)
         copy_out(0, 1, on_scalar)
         multiply(1, 2, 1)
         multiply(1, 2, 0)

from contextlib import ExitStack

import concourse.mybir as mybir
from concourse.masks import make_identity

F32 = mybir.dt.float32
BF16 = mybir.dt.bfloat16
U32 = mybir.dt.uint32
U8 = mybir.dt.uint8
FP8X4 = mybir.dt.float8_e4m3fn_x4
ACT = mybir.ActivationFunctionType
ALU = mybir.AluOpType

P = 128
BATCH = 8
STREAMS = 2
UNITS = BATCH * STREAMS
CHANNELS = 512
POSITIONS = 512
BLOCKS = CHANNELS // P
RUN = 2
GROUPS = BLOCKS // RUN
HALF_COLS = RUN * POSITIONS
PAIRS = POSITIONS // 2
HALVES = PAIRS // P
EPS = 1e-12

FLOPS = 2 * BATCH * 4 * CHANNELS * CHANNELS * POSITIONS


def tile_interfusion_pa_t_kernel(tc, x1, x2, out_0, out_1):
    nc = tc.nc
    x_views = [
        x.rearrange("b (g p r) h w -> p b g (r h w)", g=GROUPS, r=RUN) for x in (x1, x2)
    ]
    out_views = [
        o.rearrange("b (g p r) d -> p b g (r d)", g=GROUPS, r=RUN) for o in (out_0, out_1)
    ]

    with ExitStack() as stack:
        const = stack.enter_context(tc.tile_pool(name="const", bufs=1))
        x_pool = stack.enter_context(tc.tile_pool(name="x", bufs=UNITS * GROUPS))
        stat_pool = stack.enter_context(tc.tile_pool(name="stat", bufs=4))
        work_pool = stack.enter_context(tc.tile_pool(name="work", bufs=3))
        mx_pool = stack.enter_context(tc.tile_pool(name="mx", bufs=6))
        out_pool = stack.enter_context(tc.tile_pool(name="outs", bufs=12))
        word_psum = stack.enter_context(tc.psum_pool(name="word_psum", bufs=2))
        acc_psum = stack.enter_context(tc.psum_pool(name="acc_psum", bufs=6))
        stack.enter_context(tc.manual_schedule())

        x_tiles = {}
        for unit in range(UNITS):
            for g in range(GROUPS):
                x_sb = x_pool.tile([P, HALF_COLS], BF16)
                x_rows = x_views[unit % STREAMS][:, unit // STREAMS, g, :]
                if unit == 0:
                    for r in range(RUN):
                        cols = slice(r * POSITIONS, (r + 1) * POSITIONS)
                        nc.sync.dma_start(out=x_sb[:, cols], in_=x_rows[:, cols])
                else:
                    nc.sync.dma_start(out=x_sb[:], in_=x_rows)
                x_tiles[(unit, g)] = x_sb

        def x_block(unit, i):
            r = i % RUN
            return x_tiles[(unit, i // RUN)][:, r * POSITIONS : (r + 1) * POSITIONS]

        one = const.tile([P, 1], F32)
        nc.vector.memset(one[:], 1.0)
        root_of_one = const.tile([P, 1], F32)
        nc.scalar.activation(out=root_of_one[:], in_=one[:], func=ACT.Sqrt)

        plus_floor = const.tile([P, 1], F32)
        nc.vector.tensor_scalar_mul(out=plus_floor[:], in0=one[:], scalar1=EPS * EPS)
        minus_floor = const.tile([P, 1], F32)
        nc.vector.tensor_scalar_mul(out=minus_floor[:], in0=one[:], scalar1=-EPS * EPS)

        identity = const.tile([P, P], F32)
        make_identity(nc, identity[:])

        zeros = const.tile([P, CHANNELS], BF16)
        nc.gpsimd.memset(zeros[:], 0.0)

        def warm_up(count):
            idle_bank = acc_psum.tile([P, CHANNELS], F32, name="acc")
            for k in range(count):
                nc.tensor.matmul(
                    out=idle_bank[:], lhsT=zeros[:, :P], rhs=zeros[:], start=True, stop=True
                )

        sums, excesses, norms, inverses, u_tiles = {}, {}, {}, {}, {}
        word_banks, grouped_tiles, quantised, accs, stages = {}, {}, {}, {}, {}

        def square(unit, i, on_vector=False):
            if unit not in sums:
                sums[unit] = stat_pool.tile([P, BLOCKS], F32, name="sum_sq")
            x = x_block(unit, i)
            total = sums[unit][:, i : i + 1]
            if on_vector:
                squares_v = work_pool.tile([P, POSITIONS], BF16)
                nc.vector.scalar_tensor_tensor(
                    out=squares_v[:], in0=x, scalar=1.0, in1=x,
                    op0=ALU.mult, op1=ALU.mult, accum_out=total,
                )
            else:
                squares_s = work_pool.tile([P, POSITIONS], BF16)
                nc.scalar.activation(out=squares_s[:], in_=x, func=ACT.Square, accum_out=total)

        def clamp(unit):
            excesses[unit] = stat_pool.tile([P, BLOCKS], F32, name="excess")
            nc.scalar.activation(
                out=excesses[unit][:], in_=sums[unit][:], func=ACT.Relu, bias=minus_floor[:]
            )

        def norm(unit):
            norms[unit] = stat_pool.tile([P, BLOCKS], F32, name="norm_sb")
            nc.scalar.activation(
                out=norms[unit][:], in_=excesses[unit][:], func=ACT.Sqrt, bias=plus_floor[:]
            )

        def invert(unit):
            inverse = stat_pool.tile([P, BLOCKS], F32)
            nc.vector.reciprocal(out=inverse[:], in_=norms[unit][:])
            inverses[unit] = inverse

        def scale(unit):
            u_sb = work_pool.tile([P, BLOCKS, POSITIONS], BF16)
            for i in range(BLOCKS):
                nc.vector.tensor_scalar_mul(
                    out=u_sb[:, i, :],
                    in0=x_block(unit, i),
                    scalar1=inverses[unit][:, i : i + 1],
                )
            u_tiles[unit] = u_sb

        def transpose(unit):
            banks = []
            for g in range(GROUPS):
                word_bank = word_psum.tile([P, RUN, HALVES, P], F32)
                for r in range(RUN):
                    words = u_tiles[unit][:, g * RUN + r, :].bitcast(F32)
                    for h in range(HALVES):
                        nc.tensor.transpose(
                            out=word_bank[:, r, h, :],
                            in_=words[:, h * P : (h + 1) * P],
                            identity=identity[:],
                        )
                banks.append(word_bank)
            word_banks[unit] = banks

        def gather_words(unit, g, copy):
            if unit not in grouped_tiles:
                grouped_tiles[unit] = work_pool.tile(
                    [P, BLOCKS, P, HALVES * 2], BF16, name="grouped", align_bytes=64
                )
            copy(
                out=grouped_tiles[unit][:, g * RUN : (g + 1) * RUN, :, :].bitcast(F32),
                in_=word_banks[unit][g][:].rearrange("q j h c -> q j c h"),
            )

        def quantise(unit):
            codes = mx_pool.tile([P, CHANNELS], U32, align_bytes=256)
            scales = mx_pool.tile([P, CHANNELS], U8, align_bytes=256)
            nc.vector.quantize_mx(
                out=codes[:].bitcast(FP8X4),
                scales=scales[:],
                in_=grouped_tiles[unit][:].rearrange("q j c k -> q (j c k)"),
            )
            quantised[unit] = (codes, scales)

        def multiply(unit, i, left_unit):
            own, left = quantised[unit], quantised[left_unit]
            if left_unit == unit:
                accs[(unit, i)] = acc_psum.tile([P, CHANNELS], F32, name="acc")
            nc.tensor.matmul_mx(
                out=accs[(unit, i)][:],
                lhsT=left[0][:, i * P : (i + 1) * P].bitcast(FP8X4),
                lhsT_scale=left[1][:, i * P : (i + 1) * P],
                rhs=own[0][:].bitcast(FP8X4),
                rhs_scale=own[1][:],
                start=(left_unit == unit),
                stop=(left_unit != unit),
            )

        def copy_out(unit, i, copy):
            acc = accs[(unit, i)]
            g, r = i // RUN, i % RUN
            if r == 0:
                stages[(unit, g)] = out_pool.tile([P, RUN, CHANNELS], F32, name="stage")
            stage = stages[(unit, g)]
            copy(
                out=stage[:, r, :].rearrange("p (g c r) -> p g c r", g=GROUPS, r=RUN),
                in_=acc[:].rearrange("p (g r c) -> p g c r", g=GROUPS, r=RUN),
            )
            out_rows = out_views[unit % STREAMS][:, unit // STREAMS, g, :]
            if unit == UNITS - 1:
                nc.sync.dma_start(
                    out=out_rows[:, r * CHANNELS : (r + 1) * CHANNELS], in_=stage[:, r, :]
                )
            elif r == RUN - 1:
                nc.sync.dma_start(out=out_rows, in_=stage[:].rearrange("p r n -> p (r n)"))

        def last_block():
            unit, i, half = UNITS - 1, BLOCKS - 1, CHANNELS // GROUPS
            own, other = quantised[unit], quantised[unit ^ 1]
            stage = stages[(unit, GROUPS - 1)]
            for g, copy in enumerate((on_vector, on_scalar)):
                cols = slice(g * half, (g + 1) * half)
                acc = acc_psum.tile([P, half], F32)
                for left in (own, other):
                    nc.tensor.matmul_mx(
                        out=acc[:],
                        lhsT=left[0][:, i * P : (i + 1) * P].bitcast(FP8X4),
                        lhsT_scale=left[1][:, i * P : (i + 1) * P],
                        rhs=own[0][:, cols].bitcast(FP8X4),
                        rhs_scale=own[1][:, cols],
                        start=(left is own),
                        stop=(left is other),
                    )
                copy(
                    out=stage[:, RUN - 1, cols].rearrange("p (c r) -> p c r", r=RUN),
                    in_=acc[:].rearrange("p (r c) -> p c r", r=RUN),
                )
                first = (RUN - 1) * CHANNELS + g * half
                nc.sync.dma_start(
                    out=out_views[unit % STREAMS][
                        :, unit // STREAMS, GROUPS - 1, first : first + half
                    ],
                    in_=stage[:, RUN - 1, cols],
                )

        on_vector, on_scalar = nc.vector.tensor_copy, nc.scalar.copy

        warm_up(12)
        square(0, 0)
        square(0, 1, on_vector=True)
        square(0, 2)
        square(0, 3, on_vector=True)
        square(1, 0)
        square(1, 1, on_vector=True)
        clamp(0)
        square(1, 2)
        norm(0)
        square(1, 3, on_vector=True)
        invert(0)
        square(2, 0)
        square(2, 1, on_vector=True)
        scale(0)
        transpose(0)
        warm_up(3)
        square(2, 2)
        clamp(1)
        square(2, 3)
        norm(1)
        square(3, 1, on_vector=True)
        gather_words(0, 1, on_vector)
        invert(1)
        scale(1)
        gather_words(0, 0, on_scalar)
        transpose(1)
        clamp(2)
        square(3, 0)
        norm(2)
        quantise(0)
        invert(2)
        square(3, 3)
        gather_words(1, 1, on_vector)
        square(3, 2)
        multiply(0, 0, 0)
        multiply(0, 1, 0)
        multiply(0, 2, 0)
        scale(2)
        gather_words(1, 0, on_scalar)
        clamp(3)
        quantise(1)
        transpose(2)
        square(4, 0)
        norm(3)
        multiply(0, 0, 1)
        multiply(0, 1, 1)
        multiply(0, 2, 1)
        multiply(0, 3, 0)
        multiply(0, 3, 1)
        invert(3)
        scale(3)
        square(4, 1)
        gather_words(2, 0, on_vector)
        square(4, 2)
        copy_out(0, 0, on_scalar)
        multiply(1, 0, 1)
        multiply(1, 0, 0)
        gather_words(2, 1, on_vector)
        transpose(3)
        multiply(1, 1, 1)
        multiply(1, 1, 0)
        copy_out(0, 1, on_scalar)
        multiply(1, 2, 1)
        multiply(1, 2, 0)
        square(4, 3)
        copy_out(0, 2, on_vector)
        multiply(1, 3, 1)
        multiply(1, 3, 0)
        square(5, 0)
        clamp(4)
        copy_out(0, 3, on_vector)
        quantise(2)
        gather_words(3, 0, on_scalar)
        norm(4)
        gather_words(3, 1, on_scalar)
        square(5, 1)
        copy_out(1, 0, on_vector)
        invert(4)
        copy_out(1, 1, on_vector)

        for t in range(2, UNITS + 1):
            if t < UNITS:
                for i in range(BLOCKS - 1):
                    multiply(t, i, t)
            if t + 2 < UNITS:
                scale(t + 2)
                transpose(t + 2)
            if t + 1 < UNITS:
                quantise(t + 1)
            copy_out(t - 1, 2, on_scalar if t - 1 >= UNITS - 4 else on_vector)
            if t < UNITS:
                copy_out(t - 1, 3, on_scalar if t - 1 == UNITS - 4 else on_vector)
            if t + 3 < UNITS:
                square(t + 3, 2)
                square(t + 3, 3)
            if t + 4 < UNITS:
                square(t + 4, 0)
            if t + 3 < UNITS:
                clamp(t + 3)
            if t + 2 < UNITS:
                gather_words(t + 2, 0, on_vector if t + 2 >= UNITS - 2 else on_scalar)
            if t + 3 < UNITS:
                norm(t + 3)
            if t + 2 < UNITS:
                gather_words(t + 2, 1, on_scalar)
            if t + 4 < UNITS:
                square(t + 4, 1)
            if t < UNITS:
                for i in range(BLOCKS if t < UNITS - 1 else BLOCKS - 1):
                    if i == BLOCKS - 1:
                        multiply(t, i, t)
                    multiply(t, i, t ^ 1)
                copy_out(t, 0, on_scalar if t >= UNITS - 4 else on_vector)
            if t + 3 < UNITS:
                invert(t + 3)
            if t < UNITS:
                copy_out(t, 1, on_vector)
        last_block()
